import numpy as np
import ml_dtypes


def mxq(x, axis, fmt="e4m3"):
    dtype, down = {"e4m3": (ml_dtypes.float8_e4m3fn, 7), "e5m2": (ml_dtypes.float8_e5m2, 14)}[fmt]
    v = np.moveaxis(np.asarray(x, np.float32).astype(ml_dtypes.bfloat16).astype(np.float64), axis, -1)
    blocks = v.reshape(v.shape[:-1] + (-1, 32))
    amax = np.abs(blocks).max(-1, keepdims=True)
    byte = np.maximum(np.where(amax > 0, np.frexp(amax)[1] - 1 + 127, 0) - down, 1)
    scale = np.exp2(byte - 127.0)
    codes = (blocks / scale).astype(np.float32).astype(dtype).astype(np.float64)
    return np.moveaxis((codes * scale).reshape(v.shape), -1, axis)


WIDE = False


def mx_kscale(k):
    if not WIDE:
        return np.ones(k)
    levels = np.array([10, -10, 5, -5, 0])
    a = np.random.permutation(np.resize(levels, k // 512 * 4)).reshape(k // 512, 4)
    idx = np.arange(k)
    return np.exp2(a[idx // 512, idx % 128 // 32])


BF16 = ml_dtypes.bfloat16


def bf(x):
    return np.asarray(x, np.float32).astype(BF16)


def f64(x):
    return np.asarray(x).astype(np.float64)


E2M1 = np.array([0.0, 0.5, 1.0, 1.5, 2.0, 3.0, 4.0, 6.0, -0.0, -0.5, -1.0, -1.5, -2.0, -3.0, -4.0, -6.0])


def pack_weight(w, fmt):
    k, n = w.shape
    w = f64(bf(w)).reshape(k // 32, 32, n)
    amax = np.abs(w).max(1)
    if fmt == "e4m3":
        byte = np.frexp(amax)[1] - 1 + 127 - 7
    else:
        mant, ex = np.frexp(amax / 6.0)
        byte = np.where(mant > 0.5, ex, ex - 1) + 127
    byte = np.clip(np.where(amax > 0, byte, 1), 1, 254)
    scaled = (w * np.exp2(127.0 - byte)[:, None, :]).reshape(k, n).astype(np.float32)
    by_word = np.ascontiguousarray(scaled.reshape(k // 512, 128, 4, n).transpose(0, 1, 3, 2))
    if fmt == "e4m3":
        words = by_word.astype(ml_dtypes.float8_e4m3fn).view(np.uint8)
    else:
        c = by_word.astype(ml_dtypes.float4_e2m1fn).view(np.uint8) & 0xF
        words = c[..., 0::2] | (c[..., 1::2] << 4)
    return np.ascontiguousarray(words), np.ascontiguousarray(byte.astype(np.uint8).reshape(k // 512, 16, n))


def unpack_weight(words, scales, fmt):
    g, p, n, _ = words.shape
    if fmt == "e4m3":
        vals = np.ascontiguousarray(words).view(ml_dtypes.float8_e4m3fn).astype(np.float64)
    else:
        nib = np.empty((g, p, n, 4), np.uint8)
        nib[..., 0::2] = words & 0xF
        nib[..., 1::2] = words >> 4
        vals = E2M1[nib]
    vals = vals * np.repeat(np.exp2(scales.astype(np.float64) - 127.0), 8, axis=1)[..., None]
    return vals.transpose(0, 1, 3, 2).reshape(g * 512, n)


B, N, HD, ED, F = 1, 16, 256, 512, 16384
TD = HD + HD
MD = TD + ED
EPS = 1e-5
FMT = "e4m3"


def layer_norm(x, g, b):
    mu = x.mean(-1, keepdims=True)
    var = x.var(-1, keepdims=True)
    return (x - mu) * (1.0 / np.sqrt(var + EPS)) * g + b


def setup_inputs():
    t = mx_kscale(F)
    rx = mx_kscale(MD)[:HD]
    r = np.concatenate([rx, rx, np.ones(ED)])
    hid = bf(np.maximum(np.random.standard_normal((B, N, N, F)), 0.0) * t)
    x_down = bf(np.random.standard_normal((B, N, HD)) * rx)
    p_ln = bf(np.random.standard_normal((B, N, N, ED)))
    W2_words, W2_scales = pack_weight(np.random.standard_normal((F, MD)) / np.sqrt(F) / t[:, None] * r, FMT)
    b2 = bf(0.1 * np.random.standard_normal(MD) * r)
    Wo_words, Wo_scales = pack_weight(np.random.standard_normal((MD, ED)) / np.sqrt(MD) / r[:, None], FMT)
    bo = bf(0.1 * np.random.standard_normal(ED))
    ln_out_g = bf(1.0 + 0.1 * np.random.standard_normal(ED))
    ln_out_b = bf(0.1 * np.random.standard_normal(ED))
    return {"hid": hid,
            "x_down": x_down,
            "p_ln": p_ln,
            "W2_words": W2_words,
            "W2_scales": W2_scales,
            "b2": b2,
            "Wo_words": Wo_words,
            "Wo_scales": Wo_scales,
            "bo": bo,
            "ln_out_g": ln_out_g,
            "ln_out_b": ln_out_b}


def reference(hid, x_down, p_ln, W2_words, W2_scales, b2, Wo_words, Wo_scales, bo, ln_out_g, ln_out_b):
    xd, pl = f64(x_down), f64(p_ln)
    edge_bias = np.concatenate([np.broadcast_to(xd[:, :, None, :], (B, N, N, HD)),
                                np.broadcast_to(xd[:, None, :, :], (B, N, N, HD))], axis=-1)
    z_in = np.concatenate([edge_bias, pl], axis=-1)
    m = np.maximum((mxq(f64(hid), 3, "e4m3") @ unpack_weight(W2_words, W2_scales, FMT)) + f64(b2), 0.0)
    z = (mxq(m + z_in, 3, "e4m3") @ unpack_weight(Wo_words, Wo_scales, FMT)) + f64(bo)
    return pl + layer_norm(z, f64(ln_out_g), f64(ln_out_b))

@@ -1,0 +1,288 @@
+from contextlib import ExitStack
+
+import concourse.mybir as mybir
+from concourse.masks import make_identity
+
+F32 = mybir.dt.float32
+BF16 = mybir.dt.bfloat16
+I32 = mybir.dt.int32
+U32 = mybir.dt.uint32
+U8 = mybir.dt.uint8
+FP8X4 = mybir.dt.float8_e4m3fn_x4
+ALU = mybir.AluOpType
+ACT = mybir.ActivationFunctionType
+
+P = 128
+PACK = 4
+K_PASS = P * PACK
+BANK = 512
+
+ROWS = 256
+ROW_TILES = ROWS // P
+NODES = 16
+HD = 256
+K1 = 16384
+N1 = 1024
+N2 = 512
+PASSES1 = K1 // K_PASS
+PASSES2 = N1 // K_PASS
+HALVES = N1 // BANK
+EPS = 1e-5
+
+BATCH = 4
+BATCHES = PASSES1 // BATCH
+PLANES = 4
+W2_BUFS = 3 * BATCH
+
+FLOPS = 2 * ROWS * K1 * N1 + 2 * ROWS * N1 * N2
+
+
+def tile_edgeupdaterwrapper_v01_pb_k_kernel(
+    tc, hid, x_down, p_ln, W2_words, W2_scales, b2, Wo_words, Wo_scales, bo, ln_out_g, ln_out_b, out
+):
+    nc = tc.nc
+    hid_rows = hid.rearrange("b i j k -> (b i j) k").rearrange("(t p) k -> p t k", p=P)
+    p_ln_rows = p_ln.rearrange("b i j f -> (b i j) f").rearrange("(t p) f -> p t f", p=P)
+    out_rows = out.rearrange("b i j f -> (b i j) f")
+
+    with ExitStack() as ctx:
+        ctx.enter_context(tc.manual_schedule())
+        keep = ctx.enter_context(tc.tile_pool(name="keep", bufs=1))
+        raw_pool = ctx.enter_context(tc.tile_pool(name="raw", bufs=3))
+        stage = ctx.enter_context(tc.tile_pool(name="stage", bufs=2))
+        w2_pool = ctx.enter_context(tc.tile_pool(name="w2", bufs=W2_BUFS))
+        acc_pool = ctx.enter_context(tc.psum_pool(name="acc", bufs=1))
+        work = ctx.enter_context(tc.psum_pool(name="work", bufs=4))
+
+        VEC_B2, VEC_BO, VEC_G, VEC_B = 0, N1, N1 + N2, N1 + 2 * N2
+        VEC_COLS = N1 + 3 * N2
+        vec_rows = keep.tile([P, VEC_COLS], BF16)
+        ones = keep.tile([P, P], BF16)
+        eps = keep.tile([P, 1], F32)
+        nc.vector.memset(vec_rows[:], 0.0)
+        nc.vector.memset(ones[:], 1.0)
+        nc.vector.memset(eps[:], EPS)
+        nc.scalar.dma_start(out=vec_rows[0:1, VEC_B2 : VEC_B2 + N1], in_=b2.unsqueeze(0))
+        nc.scalar.dma_start(out=vec_rows[0:1, VEC_BO : VEC_BO + N2], in_=bo.unsqueeze(0))
+        nc.scalar.dma_start(out=vec_rows[0:1, VEC_G : VEC_G + N2], in_=ln_out_g.unsqueeze(0))
+        nc.scalar.dma_start(out=vec_rows[0:1, VEC_B : VEC_B + N2], in_=ln_out_b.unsqueeze(0))
+        sqrt_warm = keep.tile([P, 1], F32)
+        nc.scalar.activation(out=sqrt_warm[:], in_=eps[:], func=ACT.Sqrt)
+
+        w2_planes = keep.tile([P, BATCHES, N1], U8, align_bytes=64)
+        wo_planes = keep.tile([P, N2], U8, align_bytes=64)
+        nc.vector.memset(w2_planes[:].bitcast(I32), 0)
+        nc.vector.memset(wo_planes[:].bitcast(I32), 0)
+
+        ident_f32 = keep.tile([P, P], F32)
+        ident_bf16 = keep.tile([P, P], BF16)
+        make_identity(nc, ident_f32[:])
+        make_identity(nc, ident_bf16[:])
+
+        z_in = keep.tile([P, ROW_TILES, N1], BF16)
+        nodes_per_tile = P // NODES
+        for rt in range(ROW_TILES):
+            own = x_down[0, rt * nodes_per_tile : (rt + 1) * nodes_per_tile, :]
+            nc.gpsimd.dma_start(
+                out=z_in[:, rt, 0:HD], in_=own.unsqueeze(1).to_broadcast([nodes_per_tile, NODES, HD])
+            )
+            nc.gpsimd.dma_start(
+                out=z_in[:, rt, HD : 2 * HD],
+                in_=x_down[0, :, :].unsqueeze(0).to_broadcast([nodes_per_tile, NODES, HD]),
+            )
+        nc.gpsimd.dma_start(out=z_in[:, :, 2 * HD : N1], in_=p_ln_rows)
+
+        hid_codes = keep.tile([P, PASSES1 * ROWS], U32, align_bytes=64)
+        hid_scales = keep.tile([P, PASSES1 * ROWS], U8, align_bytes=64)
+        wo_words = keep.tile([P, PASSES2, N2], I32, align_bytes=64)
+        raw_tiles = {}
+        sorted_tiles = {}
+        grouped_tiles = {}
+        w2_tiles = {}
+        acc = {}
+        for rt in range(ROW_TILES):
+            for h in range(HALVES):
+                acc[rt, h] = acc_pool.tile([P, BANK], F32, name="acc%d%d" % (rt, h))
+
+        def load_hid(b):
+            raw = raw_pool.tile([P, ROW_TILES, BATCH * K_PASS], BF16)
+            nc.sync.dma_start(out=raw[:], in_=hid_rows[:, :, b * BATCH * K_PASS : (b + 1) * BATCH * K_PASS])
+            raw_tiles[b] = raw
+
+        def load_weights(b):
+            for quad in range(4):
+                nc.sync.dma_start(
+                    out=w2_planes[32 * quad : 32 * quad + PACK * PLANES, b, :].bitcast(I32),
+                    in_=W2_scales[b * BATCH : (b + 1) * BATCH, 4 * quad : 4 * quad + 4, :].bitcast(I32),
+                )
+            for g in range(b * BATCH, (b + 1) * BATCH):
+                w2_words = w2_pool.tile([P, N1], I32, align_bytes=64)
+                nc.sync.dma_start(out=w2_words[:], in_=W2_words[g, :, :, :].rearrange("p n t -> p (n t)").bitcast(I32))
+                w2_tiles[g] = w2_words
+
+        def sort_words(b):
+            words = stage.tile([P, ROW_TILES, BATCH, 2, P], F32, name="sorted_words")
+            nc.vector.tensor_copy(
+                out=words[:].rearrange("p t g u q -> p t g q u"),
+                in_=raw_tiles[b][:].bitcast(F32).rearrange("p t (g q u) -> p t g q u", q=P, u=2),
+            )
+            sorted_tiles[b] = words
+
+        def flip(b):
+            grouped = stage.tile([P, BATCH * ROWS * PACK], BF16, align_bytes=64, name="grouped")
+            pairs = grouped[:].bitcast(F32).rearrange("p (g r u) -> p g r u", r=ROWS, u=2)
+            for gl in range(BATCH):
+                flipped = work.tile([P, 2, ROWS], F32, tag="work", name="flipped")
+                for u in range(2):
+                    for rt in range(ROW_TILES):
+                        nc.tensor.transpose(
+                            flipped[:, u, rt * P : (rt + 1) * P], sorted_tiles[b][:, rt, gl, u, :], ident_f32[:]
+                        )
+                nc.scalar.copy(out=pairs[:, gl, :, :], in_=flipped[:].rearrange("p u r -> p r u"))
+            grouped_tiles[b] = grouped
+
+        def quantise(b):
+            cols = slice(b * BATCH * ROWS, (b + 1) * BATCH * ROWS)
+            nc.vector.quantize_mx(
+                out=hid_codes[:, cols].bitcast(FP8X4), scales=hid_scales[:, cols], in_=grouped_tiles[b][:]
+            )
+
+        def multiply(b):
+            for gl in range(BATCH):
+                g = b * BATCH + gl
+                for rt in range(ROW_TILES):
+                    rows = slice(g * ROWS + rt * P, g * ROWS + (rt + 1) * P)
+                    for h in range(HALVES):
+                        cols = slice(h * BANK, (h + 1) * BANK)
+                        nc.tensor.matmul_mx(
+                            out=acc[rt, h][:],
+                            lhsT=hid_codes[:, rows].bitcast(FP8X4),
+                            lhsT_scale=hid_scales[:, rows],
+                            rhs=w2_tiles[g][:, cols].bitcast(FP8X4),
+                            rhs_scale=w2_planes[PACK * gl : P, b, cols],
+                            start=(g == 0),
+                            stop=(g == PASSES1 - 1),
+                        )
+
+        load_hid(0)
+        load_hid(1)
+        load_weights(0)
+        nc.sync.dma_start(out=wo_words[:], in_=Wo_words.rearrange("g p n t -> p g (n t)").bitcast(I32))
+        for quad in range(4):
+            nc.sync.dma_start(
+                out=wo_planes[32 * quad : 32 * quad + PACK * PASSES2, :].bitcast(I32),
+                in_=Wo_scales[:, 4 * quad : 4 * quad + 4, :].bitcast(I32),
+            )
+
+        spread = keep.tile([P, VEC_COLS], F32)
+        for c in range(0, VEC_COLS, BANK):
+            row_bank = work.tile([P, BANK], F32, tag="work", name="row_bank")
+            nc.tensor.matmul(out=row_bank[:], lhsT=ones[:], rhs=vec_rows[:, c : c + BANK], start=True, stop=True)
+            nc.scalar.copy(out=spread[:, c : c + BANK], in_=row_bank[:])
+
+        sort_words(0)
+        flip(0)
+        sort_words(1)
+        quantise(0)
+        for b in range(BATCHES):
+            if b + 2 < BATCHES:
+                load_hid(b + 2)
+            if b + 1 < BATCHES:
+                load_weights(b + 1)
+                flip(b + 1)
+            multiply(b)
+            if b + 2 < BATCHES:
+                sort_words(b + 2)
+            if b + 1 < BATCHES:
+                quantise(b + 1)
+
+        bias_z = keep.tile([P, ROW_TILES, N1], F32)
+        shift = keep.tile([P, ROW_TILES, N2], F32)
+        for rt in range(ROW_TILES):
+            nc.vector.tensor_tensor(
+                out=bias_z[:, rt, :], in0=spread[:, VEC_B2 : VEC_B2 + N1], in1=z_in[:, rt, :], op=ALU.add
+            )
+            nc.vector.tensor_tensor(
+                out=shift[:, rt, :], in0=spread[:, VEC_B : VEC_B + N2], in1=z_in[:, rt, 2 * HD : N1], op=ALU.add
+            )
+
+        s_sorted = keep.tile([P, ROW_TILES, HALVES, PACK, P], BF16)
+        s_grouped = keep.tile([P, HALVES, ROW_TILES, P * PACK], BF16, align_bytes=64)
+        s_codes = keep.tile([P, HALVES, ROWS], U32, align_bytes=64)
+        s_scales = keep.tile([P, HALVES, ROWS], U8, align_bytes=64)
+        units = [(h, rt) for h in range(HALVES) for rt in range(ROW_TILES)]
+
+        def finish_s(h, rt):
+            cols = slice(h * BANK, (h + 1) * BANK)
+            summed = stage.tile([P, BANK], F32, name="summed")
+            nc.vector.tensor_tensor(out=summed[:], in0=acc[rt, h][:], in1=bias_z[:, rt, cols], op=ALU.add)
+            nc.vector.tensor_tensor(
+                out=s_sorted[:, rt, h, :, :].rearrange("p t q -> p q t"),
+                in0=summed[:].rearrange("p (q t) -> p q t", t=PACK),
+                in1=z_in[:, rt, cols].rearrange("p (q t) -> p q t", t=PACK),
+                op=ALU.max,
+            )
+            s_flipped = work.tile([P, PACK, P], BF16, tag="work", name="s_flipped")
+            for t in range(PACK):
+                nc.tensor.transpose(s_flipped[:, t, :], s_sorted[:, rt, h, t, :], ident_bf16[:])
+            nc.scalar.copy(
+                out=s_grouped[:, h, rt, :].rearrange("p (r t) -> p r t", t=PACK),
+                in_=s_flipped[:].rearrange("p t r -> p r t"),
+            )
+
+        def quantise_s(h, rt):
+            rows = slice(rt * P, (rt + 1) * P)
+            nc.vector.quantize_mx(
+                out=s_codes[:, h, rows].bitcast(FP8X4), scales=s_scales[:, h, rows], in_=s_grouped[:, h, rt, :]
+            )
+
+        for i in range(len(units)):
+            finish_s(*units[i])
+            if i > 0:
+                quantise_s(*units[i - 1])
+        quantise_s(*units[-1])
+
+        z_tiles = {}
+        stats = {}
+        for rt in range(ROW_TILES):
+            rows = slice(rt * P, (rt + 1) * P)
+            z_acc = work.tile([P, N2], F32, tag="work", name="z_acc")
+            for h in range(PASSES2):
+                nc.tensor.matmul_mx(
+                    out=z_acc[:],
+                    lhsT=s_codes[:, h, rows].bitcast(FP8X4),
+                    lhsT_scale=s_scales[:, h, rows],
+                    rhs=wo_words[:, h, :].bitcast(FP8X4),
+                    rhs_scale=wo_planes[PACK * h : P, :],
+                    start=(h == 0),
+                    stop=(h == PASSES2 - 1),
+                )
+            z = keep.tile([P, N2], F32, name="z%d" % rt)
+            nc.vector.tensor_tensor(out=z[:], in0=z_acc[:], in1=spread[:, VEC_BO : VEC_BO + N2], op=ALU.add)
+            six = keep.tile([P, 6], F32, name="six%d" % rt)
+            mean_var = keep.tile([P, 2], F32, name="mean_var%d" % rt)
+            std = keep.tile([P, 1], F32, name="std%d" % rt)
+            nc.vector.bn_stats(out=six[:], in_=z[:])
+            nc.vector.bn_aggr(out=mean_var[:], in_=six[:])
+            nc.scalar.activation(out=std[:], in_=mean_var[:, 1:2], func=ACT.Sqrt, bias=eps[:], scale=1.0)
+            z_tiles[rt] = z
+            stats[rt] = (mean_var, std)
+
+        for rt in range(ROW_TILES):
+            mean_var, std = stats[rt]
+            centred = keep.tile([P, N2], F32, name="centred%d" % rt)
+            rstd = keep.tile([P, 1], F32, name="rstd%d" % rt)
+            result = keep.tile([P, N2], F32, name="result%d" % rt)
+            nc.vector.scalar_tensor_tensor(
+                out=centred[:],
+                in0=z_tiles[rt][:],
+                scalar=mean_var[:, 0:1],
+                in1=spread[:, VEC_G : VEC_G + N2],
+                op0=ALU.subtract,
+                op1=ALU.mult,
+            )
+            nc.vector.reciprocal(out=rstd[:], in_=std[:])
+            nc.vector.scalar_tensor_tensor(
+                out=result[:], in0=centred[:], scalar=rstd[:], in1=shift[:, rt, :], op0=ALU.mult, op1=ALU.add
+            )
+            nc.sync.dma_start(out=out_rows[rt * P : (rt + 1) * P, :], in_=result[:])

@@ -33,6 +33,8 @@ BATCH = 4
 BATCHES = PASSES1 // BATCH
 PLANES = 4
 W2_BUFS = 3 * BATCH
+LATE_BATCHES = 2
+MAIN_BATCHES = BATCHES - LATE_BATCHES
 
 FLOPS = 2 * ROWS * K1 * N1 + 2 * ROWS * N1 * N2
 
@@ -109,16 +111,26 @@ def tile_edgeupdaterwrapper_v01_pb_k_kernel(
             nc.sync.dma_start(out=raw[:], in_=hid_rows[:, :, b * BATCH * K_PASS : (b + 1) * BATCH * K_PASS])
             raw_tiles[b] = raw
 
-        def load_weights(b):
+        def own_halves(b):
+            return range(HALVES) if b < MAIN_BATCHES else range(1)
+
+        def load_scales(b):
             for quad in range(4):
                 nc.sync.dma_start(
                     out=w2_planes[32 * quad : 32 * quad + PACK * PLANES, b, :].bitcast(I32),
                     in_=W2_scales[b * BATCH : (b + 1) * BATCH, 4 * quad : 4 * quad + 4, :].bitcast(I32),
                 )
+
+        def load_words(b, halves):
+            cols = slice(halves[0] * BANK, (halves[-1] + 1) * BANK)
             for g in range(b * BATCH, (b + 1) * BATCH):
-                w2_words = w2_pool.tile([P, N1], I32, align_bytes=64)
-                nc.sync.dma_start(out=w2_words[:], in_=W2_words[g, :, :, :].rearrange("p n t -> p (n t)").bitcast(I32))
-                w2_tiles[g] = w2_words
+                if g not in w2_tiles:
+                    w2_words = w2_pool.tile([P, N1], I32, align_bytes=64)
+                    w2_tiles[g] = w2_words
+                nc.sync.dma_start(
+                    out=w2_tiles[g][:, cols],
+                    in_=W2_words[g, :, cols, :].rearrange("p n t -> p (n t)").bitcast(I32),
+                )
 
         def sort_words(b):
             words = stage.tile([P, ROW_TILES, BATCH, 2, P], F32, name="sorted_words")
@@ -147,12 +159,12 @@ def tile_edgeupdaterwrapper_v01_pb_k_kernel(
                 out=hid_codes[:, cols].bitcast(FP8X4), scales=hid_scales[:, cols], in_=grouped_tiles[b][:]
             )
 
-        def multiply(b):
+        def multiply(b, halves):
             for gl in range(BATCH):
                 g = b * BATCH + gl
                 for rt in range(ROW_TILES):
                     rows = slice(g * ROWS + rt * P, g * ROWS + (rt + 1) * P)
-                    for h in range(HALVES):
+                    for h in halves:
                         cols = slice(h * BANK, (h + 1) * BANK)
                         nc.tensor.matmul_mx(
                             out=acc[rt, h][:],
@@ -166,7 +178,8 @@ def tile_edgeupdaterwrapper_v01_pb_k_kernel(
 
         load_hid(0)
         load_hid(1)
-        load_weights(0)
+        load_scales(0)
+        load_words(0, own_halves(0))
         nc.sync.dma_start(out=wo_words[:], in_=Wo_words.rearrange("g p n t -> p g (n t)").bitcast(I32))
         for quad in range(4):
             nc.sync.dma_start(
@@ -188,13 +201,18 @@ def tile_edgeupdaterwrapper_v01_pb_k_kernel(
             if b + 2 < BATCHES:
                 load_hid(b + 2)
             if b + 1 < BATCHES:
-                load_weights(b + 1)
+                load_scales(b + 1)
+                load_words(b + 1, own_halves(b + 1))
                 flip(b + 1)
-            multiply(b)
+            multiply(b, own_halves(b))
             if b + 2 < BATCHES:
                 sort_words(b + 2)
             if b + 1 < BATCHES:
                 quantise(b + 1)
+
+        late = range(MAIN_BATCHES, BATCHES)
+        for b in late:
+            load_words(b, range(1, HALVES))
 
         bias_z = keep.tile([P, ROW_TILES, N1], F32)
         shift = keep.tile([P, ROW_TILES, N2], F32)
@@ -210,7 +228,6 @@ def tile_edgeupdaterwrapper_v01_pb_k_kernel(
         s_grouped = keep.tile([P, HALVES, ROW_TILES, P * PACK], BF16, align_bytes=64)
         s_codes = keep.tile([P, HALVES, ROWS], U32, align_bytes=64)
         s_scales = keep.tile([P, HALVES, ROWS], U8, align_bytes=64)
-        units = [(h, rt) for h in range(HALVES) for rt in range(ROW_TILES)]
 
         def finish_s(h, rt):
             cols = slice(h * BANK, (h + 1) * BANK)
@@ -236,20 +253,15 @@ def tile_edgeupdaterwrapper_v01_pb_k_kernel(
                 out=s_codes[:, h, rows].bitcast(FP8X4), scales=s_scales[:, h, rows], in_=s_grouped[:, h, rt, :]
             )
 
-        for i in range(len(units)):
-            finish_s(*units[i])
-            if i > 0:
-                quantise_s(*units[i - 1])
-        quantise_s(*units[-1])
+        z_acc = {}
 
-        z_tiles = {}
-        stats = {}
-        for rt in range(ROW_TILES):
-            rows = slice(rt * P, (rt + 1) * P)
-            z_acc = work.tile([P, N2], F32, tag="work", name="z_acc")
-            for h in range(PASSES2):
+        def second_product(h):
+            for rt in range(ROW_TILES):
+                rows = slice(rt * P, (rt + 1) * P)
+                if h == 0:
+                    z_acc[rt] = work.tile([P, N2], F32, tag="work", name="z_acc")
                 nc.tensor.matmul_mx(
-                    out=z_acc[:],
+                    out=z_acc[rt][:],
                     lhsT=s_codes[:, h, rows].bitcast(FP8X4),
                     lhsT_scale=s_scales[:, h, rows],
                     rhs=wo_words[:, h, :].bitcast(FP8X4),
@@ -257,28 +269,55 @@ def tile_edgeupdaterwrapper_v01_pb_k_kernel(
                     start=(h == 0),
                     stop=(h == PASSES2 - 1),
                 )
+
+        multiply(late[0], range(1, HALVES))
+        for h in range(HALVES):
+            for rt in range(ROW_TILES):
+                finish_s(h, rt)
+            for rt in range(ROW_TILES):
+                quantise_s(h, rt)
+            if h == 0:
+                for b in late[1:]:
+                    multiply(b, range(1, HALVES))
+            second_product(h)
+
+        z_tiles = {}
+        stats = {}
+        for rt in range(ROW_TILES):
             z = keep.tile([P, N2], F32, name="z%d" % rt)
-            nc.vector.tensor_tensor(out=z[:], in0=z_acc[:], in1=spread[:, VEC_BO : VEC_BO + N2], op=ALU.add)
-            six = keep.tile([P, 6], F32, name="six%d" % rt)
-            mean_var = keep.tile([P, 2], F32, name="mean_var%d" % rt)
+            z_sum = keep.tile([P, 1], F32, name="z_sum%d" % rt)
+            neg_mean = keep.tile([P, 1], F32, name="neg_mean%d" % rt)
+            squares = keep.tile([P, N2], F32, name="squares%d" % rt)
+            square_sum = keep.tile([P, 1], F32, name="square_sum%d" % rt)
             std = keep.tile([P, 1], F32, name="std%d" % rt)
-            nc.vector.bn_stats(out=six[:], in_=z[:])
-            nc.vector.bn_aggr(out=mean_var[:], in_=six[:])
-            nc.scalar.activation(out=std[:], in_=mean_var[:, 1:2], func=ACT.Sqrt, bias=eps[:], scale=1.0)
+            nc.vector.scalar_tensor_tensor(
+                out=z[:],
+                in0=z_acc[rt][:],
+                scalar=1.0,
+                in1=spread[:, VEC_BO : VEC_BO + N2],
+                op0=ALU.mult,
+                op1=ALU.add,
+                accum_out=z_sum[:],
+            )
+            nc.vector.tensor_scalar_mul(out=neg_mean[:], in0=z_sum[:], scalar1=-1.0 / N2)
+            nc.scalar.activation(
+                out=squares[:], in_=z[:], func=ACT.Square, bias=neg_mean[:], scale=1.0, accum_out=square_sum[:]
+            )
+            nc.scalar.activation(out=std[:], in_=square_sum[:], func=ACT.Sqrt, bias=eps[:], scale=1.0 / N2)
             z_tiles[rt] = z
-            stats[rt] = (mean_var, std)
+            stats[rt] = (neg_mean, std)
 
         for rt in range(ROW_TILES):
-            mean_var, std = stats[rt]
+            neg_mean, std = stats[rt]
             centred = keep.tile([P, N2], F32, name="centred%d" % rt)
             rstd = keep.tile([P, 1], F32, name="rstd%d" % rt)
             result = keep.tile([P, N2], F32, name="result%d" % rt)
             nc.vector.scalar_tensor_tensor(
                 out=centred[:],
                 in0=z_tiles[rt][:],
-                scalar=mean_var[:, 0:1],
+                scalar=neg_mean[:],
                 in1=spread[:, VEC_G : VEC_G + N2],
-                op0=ALU.subtract,
+                op0=ALU.add,
                 op1=ALU.mult,
             )
             nc.vector.reciprocal(out=rstd[:], in_=std[:])

@@ -35,6 +35,7 @@ PLANES = 4
 W2_BUFS = 3 * BATCH
 LATE_BATCHES = 2
 MAIN_BATCHES = BATCHES - LATE_BATCHES
+HID_LEAD = 3
 
 FLOPS = 2 * ROWS * K1 * N1 + 2 * ROWS * N1 * N2
 
@@ -50,7 +51,7 @@ def tile_edgeupdaterwrapper_v01_pb_k_kernel(
     with ExitStack() as ctx:
         ctx.enter_context(tc.manual_schedule())
         keep = ctx.enter_context(tc.tile_pool(name="keep", bufs=1))
-        raw_pool = ctx.enter_context(tc.tile_pool(name="raw", bufs=3))
+        raw_pool = ctx.enter_context(tc.tile_pool(name="raw", bufs=HID_LEAD + 1))
         stage = ctx.enter_context(tc.tile_pool(name="stage", bufs=2))
         w2_pool = ctx.enter_context(tc.tile_pool(name="w2", bufs=W2_BUFS))
         acc_pool = ctx.enter_context(tc.psum_pool(name="acc", bufs=1))
@@ -176,8 +177,8 @@ def tile_edgeupdaterwrapper_v01_pb_k_kernel(
                             stop=(g == PASSES1 - 1),
                         )
 
-        load_hid(0)
-        load_hid(1)
+        for b in range(HID_LEAD):
+            load_hid(b)
         load_scales(0)
         load_words(0, own_halves(0))
         nc.sync.dma_start(out=wo_words[:], in_=Wo_words.rearrange("g p n t -> p g (n t)").bitcast(I32))
@@ -198,8 +199,8 @@ def tile_edgeupdaterwrapper_v01_pb_k_kernel(
         sort_words(1)
         quantise(0)
         for b in range(BATCHES):
-            if b + 2 < BATCHES:
-                load_hid(b + 2)
+            if b + HID_LEAD < BATCHES:
+                load_hid(b + HID_LEAD)
             if b + 1 < BATCHES:
                 load_scales(b + 1)
                 load_words(b + 1, own_halves(b + 1))
@@ -287,7 +288,7 @@ def tile_edgeupdaterwrapper_v01_pb_k_kernel(
             z = keep.tile([P, N2], F32, name="z%d" % rt)
             z_sum = keep.tile([P, 1], F32, name="z_sum%d" % rt)
             neg_mean = keep.tile([P, 1], F32, name="neg_mean%d" % rt)
-            squares = keep.tile([P, N2], F32, name="squares%d" % rt)
+            result = keep.tile([P, N2], F32, name="result%d" % rt)
             square_sum = keep.tile([P, 1], F32, name="square_sum%d" % rt)
             std = keep.tile([P, 1], F32, name="std%d" % rt)
             nc.vector.scalar_tensor_tensor(
@@ -301,17 +302,16 @@ def tile_edgeupdaterwrapper_v01_pb_k_kernel(
             )
             nc.vector.tensor_scalar_mul(out=neg_mean[:], in0=z_sum[:], scalar1=-1.0 / N2)
             nc.scalar.activation(
-                out=squares[:], in_=z[:], func=ACT.Square, bias=neg_mean[:], scale=1.0, accum_out=square_sum[:]
+                out=result[:], in_=z[:], func=ACT.Square, bias=neg_mean[:], scale=1.0, accum_out=square_sum[:]
             )
             nc.scalar.activation(out=std[:], in_=square_sum[:], func=ACT.Sqrt, bias=eps[:], scale=1.0 / N2)
             z_tiles[rt] = z
-            stats[rt] = (neg_mean, std)
+            stats[rt] = (neg_mean, std, result)
 
         for rt in range(ROW_TILES):
-            neg_mean, std = stats[rt]
+            neg_mean, std, result = stats[rt]
             centred = keep.tile([P, N2], F32, name="centred%d" % rt)
             rstd = keep.tile([P, 1], F32, name="rstd%d" % rt)
-            result = keep.tile([P, N2], F32, name="result%d" % rt)
             nc.vector.scalar_tensor_tensor(
                 out=centred[:],
                 in0=z_tiles[rt][:],

@@ -35,7 +35,7 @@ PLANES = 4
 W2_BUFS = 3 * BATCH
 LATE_BATCHES = 2
 MAIN_BATCHES = BATCHES - LATE_BATCHES
-HID_LEAD = 3
+HID_LEAD = 2
 
 FLOPS = 2 * ROWS * K1 * N1 + 2 * ROWS * N1 * N2
 
@@ -57,6 +57,11 @@ def tile_edgeupdaterwrapper_v01_pb_k_kernel(
         acc_pool = ctx.enter_context(tc.psum_pool(name="acc", bufs=1))
         work = ctx.enter_context(tc.psum_pool(name="work", bufs=4))
 
+        w2_planes = keep.tile([P, BATCHES, N1], U8, align_bytes=64)
+        wo_planes = keep.tile([P, N2], U8, align_bytes=64)
+        nc.vector.memset(w2_planes[:].bitcast(I32), 0)
+        nc.vector.memset(wo_planes[:].bitcast(I32), 0)
+
         VEC_B2, VEC_BO, VEC_G, VEC_B = 0, N1, N1 + N2, N1 + 2 * N2
         VEC_COLS = N1 + 3 * N2
         vec_rows = keep.tile([P, VEC_COLS], BF16)
@@ -72,15 +77,17 @@ def tile_edgeupdaterwrapper_v01_pb_k_kernel(
         sqrt_warm = keep.tile([P, 1], F32)
         nc.scalar.activation(out=sqrt_warm[:], in_=eps[:], func=ACT.Sqrt)
 
-        w2_planes = keep.tile([P, BATCHES, N1], U8, align_bytes=64)
-        wo_planes = keep.tile([P, N2], U8, align_bytes=64)
-        nc.vector.memset(w2_planes[:].bitcast(I32), 0)
-        nc.vector.memset(wo_planes[:].bitcast(I32), 0)
-
         ident_f32 = keep.tile([P, P], F32)
         ident_bf16 = keep.tile([P, P], BF16)
         make_identity(nc, ident_f32[:])
         make_identity(nc, ident_bf16[:])
+
+        for b in range(BATCHES):
+            for quad in range(4):
+                nc.gpsimd.dma_start(
+                    out=w2_planes[32 * quad : 32 * quad + PACK * PLANES, b, :].bitcast(F32),
+                    in_=W2_scales[b * BATCH : (b + 1) * BATCH, 4 * quad : 4 * quad + 4, :].bitcast(F32),
+                )
 
         z_in = keep.tile([P, ROW_TILES, N1], BF16)
         nodes_per_tile = P // NODES
@@ -114,13 +121,6 @@ def tile_edgeupdaterwrapper_v01_pb_k_kernel(
 
         def own_halves(b):
             return range(HALVES) if b < MAIN_BATCHES else range(1)
-
-        def load_scales(b):
-            for quad in range(4):
-                nc.sync.dma_start(
-                    out=w2_planes[32 * quad : 32 * quad + PACK * PLANES, b, :].bitcast(I32),
-                    in_=W2_scales[b * BATCH : (b + 1) * BATCH, 4 * quad : 4 * quad + 4, :].bitcast(I32),
-                )
 
         def load_words(b, halves):
             cols = slice(halves[0] * BANK, (halves[-1] + 1) * BANK)
@@ -179,14 +179,7 @@ def tile_edgeupdaterwrapper_v01_pb_k_kernel(
 
         for b in range(HID_LEAD):
             load_hid(b)
-        load_scales(0)
         load_words(0, own_halves(0))
-        nc.sync.dma_start(out=wo_words[:], in_=Wo_words.rearrange("g p n t -> p g (n t)").bitcast(I32))
-        for quad in range(4):
-            nc.sync.dma_start(
-                out=wo_planes[32 * quad : 32 * quad + PACK * PASSES2, :].bitcast(I32),
-                in_=Wo_scales[:, 4 * quad : 4 * quad + 4, :].bitcast(I32),
-            )
 
         spread = keep.tile([P, VEC_COLS], F32)
         for c in range(0, VEC_COLS, BANK):
@@ -202,7 +195,6 @@ def tile_edgeupdaterwrapper_v01_pb_k_kernel(
             if b + HID_LEAD < BATCHES:
                 load_hid(b + HID_LEAD)
             if b + 1 < BATCHES:
-                load_scales(b + 1)
                 load_words(b + 1, own_halves(b + 1))
                 flip(b + 1)
             multiply(b, own_halves(b))
@@ -211,6 +203,12 @@ def tile_edgeupdaterwrapper_v01_pb_k_kernel(
             if b + 1 < BATCHES:
                 quantise(b + 1)
 
+        nc.sync.dma_start(out=wo_words[:], in_=Wo_words.rearrange("g p n t -> p g (n t)").bitcast(I32))
+        for quad in range(4):
+            nc.sync.dma_start(
+                out=wo_planes[32 * quad : 32 * quad + PACK * PASSES2, :].bitcast(I32),
+                in_=Wo_scales[:, 4 * quad : 4 * quad + 4, :].bitcast(I32),
+            )
         late = range(MAIN_BATCHES, BATCHES)
         for b in late:
             load_words(b, range(1, HALVES))

@@ -37,6 +37,8 @@ LATE_BATCHES = 2
 MAIN_BATCHES = BATCHES - LATE_BATCHES
 HID_LEAD = 2
 
+SPREAD_AFTER = 2
+
 FLOPS = 2 * ROWS * K1 * N1 + 2 * ROWS * N1 * N2
 
 
@@ -59,6 +61,10 @@ def tile_edgeupdaterwrapper_v01_pb_k_kernel(
 
         w2_planes = keep.tile([P, BATCHES, N1], U8, align_bytes=64)
         wo_planes = keep.tile([P, N2], U8, align_bytes=64)
+        eps = keep.tile([P, 1], F32)
+        nc.vector.memset(eps[:], EPS)
+        sqrt_warm = keep.tile([P, 1], F32)
+        nc.scalar.activation(out=sqrt_warm[:], in_=eps[:], func=ACT.Sqrt)
         nc.vector.memset(w2_planes[:].bitcast(I32), 0)
         nc.vector.memset(wo_planes[:].bitcast(I32), 0)
 
@@ -66,16 +72,12 @@ def tile_edgeupdaterwrapper_v01_pb_k_kernel(
         VEC_COLS = N1 + 3 * N2
         vec_rows = keep.tile([P, VEC_COLS], BF16)
         ones = keep.tile([P, P], BF16)
-        eps = keep.tile([P, 1], F32)
         nc.vector.memset(vec_rows[:], 0.0)
         nc.vector.memset(ones[:], 1.0)
-        nc.vector.memset(eps[:], EPS)
         nc.scalar.dma_start(out=vec_rows[0:1, VEC_B2 : VEC_B2 + N1], in_=b2.unsqueeze(0))
         nc.scalar.dma_start(out=vec_rows[0:1, VEC_BO : VEC_BO + N2], in_=bo.unsqueeze(0))
         nc.scalar.dma_start(out=vec_rows[0:1, VEC_G : VEC_G + N2], in_=ln_out_g.unsqueeze(0))
         nc.scalar.dma_start(out=vec_rows[0:1, VEC_B : VEC_B + N2], in_=ln_out_b.unsqueeze(0))
-        sqrt_warm = keep.tile([P, 1], F32)
-        nc.scalar.activation(out=sqrt_warm[:], in_=eps[:], func=ACT.Sqrt)
 
         ident_f32 = keep.tile([P, P], F32)
         ident_bf16 = keep.tile([P, P], BF16)
@@ -160,6 +162,14 @@ def tile_edgeupdaterwrapper_v01_pb_k_kernel(
                 out=hid_codes[:, cols].bitcast(FP8X4), scales=hid_scales[:, cols], in_=grouped_tiles[b][:]
             )
 
+        spread = keep.tile([P, VEC_COLS], F32)
+
+        def spread_vectors():
+            for c in range(0, VEC_COLS, BANK):
+                row_bank = work.tile([P, BANK], F32, tag="work", name="row_bank")
+                nc.tensor.matmul(out=row_bank[:], lhsT=ones[:], rhs=vec_rows[:, c : c + BANK], start=True, stop=True)
+                nc.scalar.copy(out=spread[:, c : c + BANK], in_=row_bank[:])
+
         def multiply(b, halves):
             for gl in range(BATCH):
                 g = b * BATCH + gl
@@ -181,12 +191,6 @@ def tile_edgeupdaterwrapper_v01_pb_k_kernel(
             load_hid(b)
         load_words(0, own_halves(0))
 
-        spread = keep.tile([P, VEC_COLS], F32)
-        for c in range(0, VEC_COLS, BANK):
-            row_bank = work.tile([P, BANK], F32, tag="work", name="row_bank")
-            nc.tensor.matmul(out=row_bank[:], lhsT=ones[:], rhs=vec_rows[:, c : c + BANK], start=True, stop=True)
-            nc.scalar.copy(out=spread[:, c : c + BANK], in_=row_bank[:])
-
         sort_words(0)
         flip(0)
         sort_words(1)
@@ -198,6 +202,8 @@ def tile_edgeupdaterwrapper_v01_pb_k_kernel(
                 load_words(b + 1, own_halves(b + 1))
                 flip(b + 1)
             multiply(b, own_halves(b))
+            if b == SPREAD_AFTER:
+                spread_vectors()
             if b + 2 < BATCHES:
                 sort_words(b + 2)
             if b + 1 < BATCHES:

@@ -35,7 +35,7 @@ PLANES = 4
 W2_BUFS = 3 * BATCH
 LATE_BATCHES = 2
 MAIN_BATCHES = BATCHES - LATE_BATCHES
-HID_LEAD = 2
+HID_LEAD = 3
 
 SPREAD_AFTER = 2
 
@@ -194,20 +194,24 @@ def tile_edgeupdaterwrapper_v01_pb_k_kernel(
         sort_words(0)
         flip(0)
         sort_words(1)
+        flip(1)
         quantise(0)
+        sort_words(2)
+        quantise(1)
         for b in range(BATCHES):
             if b + HID_LEAD < BATCHES:
                 load_hid(b + HID_LEAD)
             if b + 1 < BATCHES:
                 load_words(b + 1, own_halves(b + 1))
-                flip(b + 1)
+            if b + 2 < BATCHES:
+                flip(b + 2)
             multiply(b, own_halves(b))
             if b == SPREAD_AFTER:
                 spread_vectors()
+            if b + 3 < BATCHES:
+                sort_words(b + 3)
             if b + 2 < BATCHES:
-                sort_words(b + 2)
-            if b + 1 < BATCHES:
-                quantise(b + 1)
+                quantise(b + 2)
 
         nc.sync.dma_start(out=wo_words[:], in_=Wo_words.rearrange("g p n t -> p g (n t)").bitcast(I32))
         for quad in range(4):

@@ -21,6 +21,7 @@ ROWS = 256
 ROW_TILES = ROWS // P
 NODES = 16
 HD = 256
+TD = 2 * HD
 K1 = 16384
 N1 = 1024
 N2 = 512
@@ -63,8 +64,8 @@ def tile_edgeupdaterwrapper_v01_pb_k_kernel(
         wo_planes = keep.tile([P, N2], U8, align_bytes=64)
         eps = keep.tile([P, 1], F32)
         nc.vector.memset(eps[:], EPS)
-        sqrt_warm = keep.tile([P, 1], F32)
-        nc.scalar.activation(out=sqrt_warm[:], in_=eps[:], func=ACT.Sqrt)
+        table_warm = keep.tile([P, 1], F32)
+        nc.scalar.activation(out=table_warm[:], in_=eps[:], func=ACT.Abs_reciprocal_sqrt)
         nc.vector.memset(w2_planes[:].bitcast(I32), 0)
         nc.vector.memset(wo_planes[:].bitcast(I32), 0)
 
@@ -72,12 +73,15 @@ def tile_edgeupdaterwrapper_v01_pb_k_kernel(
         VEC_COLS = N1 + 3 * N2
         vec_rows = keep.tile([P, VEC_COLS], BF16)
         ones = keep.tile([P, P], BF16)
+        node_rows = keep.tile([P, HD], BF16)
+        nc.vector.memset(node_rows[:], 0.0)
         nc.vector.memset(vec_rows[:], 0.0)
         nc.vector.memset(ones[:], 1.0)
         nc.scalar.dma_start(out=vec_rows[0:1, VEC_B2 : VEC_B2 + N1], in_=b2.unsqueeze(0))
         nc.scalar.dma_start(out=vec_rows[0:1, VEC_BO : VEC_BO + N2], in_=bo.unsqueeze(0))
         nc.scalar.dma_start(out=vec_rows[0:1, VEC_G : VEC_G + N2], in_=ln_out_g.unsqueeze(0))
         nc.scalar.dma_start(out=vec_rows[0:1, VEC_B : VEC_B + N2], in_=ln_out_b.unsqueeze(0))
+        nc.scalar.dma_start(out=node_rows[0:NODES, :], in_=x_down[0, :, :])
 
         ident_f32 = keep.tile([P, P], F32)
         ident_bf16 = keep.tile([P, P], BF16)
@@ -92,17 +96,7 @@ def tile_edgeupdaterwrapper_v01_pb_k_kernel(
                 )
 
         z_in = keep.tile([P, ROW_TILES, N1], BF16)
-        nodes_per_tile = P // NODES
-        for rt in range(ROW_TILES):
-            own = x_down[0, rt * nodes_per_tile : (rt + 1) * nodes_per_tile, :]
-            nc.gpsimd.dma_start(
-                out=z_in[:, rt, 0:HD], in_=own.unsqueeze(1).to_broadcast([nodes_per_tile, NODES, HD])
-            )
-            nc.gpsimd.dma_start(
-                out=z_in[:, rt, HD : 2 * HD],
-                in_=x_down[0, :, :].unsqueeze(0).to_broadcast([nodes_per_tile, NODES, HD]),
-            )
-        nc.gpsimd.dma_start(out=z_in[:, :, 2 * HD : N1], in_=p_ln_rows)
+        nc.gpsimd.dma_start(out=z_in[:, :, TD:N1], in_=p_ln_rows)
 
         hid_codes = keep.tile([P, PASSES1 * ROWS], U32, align_bytes=64)
         hid_scales = keep.tile([P, PASSES1 * ROWS], U8, align_bytes=64)
@@ -162,13 +156,41 @@ def tile_edgeupdaterwrapper_v01_pb_k_kernel(
                 out=hid_codes[:, cols].bitcast(FP8X4), scales=hid_scales[:, cols], in_=grouped_tiles[b][:]
             )
 
-        spread = keep.tile([P, VEC_COLS], F32)
+        bias_z = keep.tile([P, ROW_TILES, N1], F32)
+        spread = keep.tile([P, VEC_COLS - TD], F32)
+        pick_i = keep.tile([P, ROW_TILES, P], BF16)
+        pick_j = keep.tile([P, P], BF16)
+        nodes_per_tile = P // NODES
+
+        def make_picks():
+            nc.vector.tensor_copy(
+                out=pick_j[:].rearrange("n (a c) -> n a c", c=NODES),
+                in_=ident_bf16[:, 0:NODES].unsqueeze(1).to_broadcast([P, nodes_per_tile, NODES]),
+            )
+            for rt in range(ROW_TILES):
+                own = ident_bf16[:, rt * nodes_per_tile : (rt + 1) * nodes_per_tile]
+                nc.vector.tensor_copy(
+                    out=pick_i[:, rt, :].rearrange("n (a c) -> n a c", c=NODES),
+                    in_=own.unsqueeze(2).to_broadcast([P, nodes_per_tile, NODES]),
+                )
 
         def spread_vectors():
-            for c in range(0, VEC_COLS, BANK):
+            for c in range(TD, VEC_COLS, BANK):
                 row_bank = work.tile([P, BANK], F32, tag="work", name="row_bank")
                 nc.tensor.matmul(out=row_bank[:], lhsT=ones[:], rhs=vec_rows[:, c : c + BANK], start=True, stop=True)
-                nc.scalar.copy(out=spread[:, c : c + BANK], in_=row_bank[:])
+                nc.scalar.copy(out=spread[:, c - TD : c - TD + BANK], in_=row_bank[:])
+            for rt in range(ROW_TILES):
+                node_bank = work.tile([P, TD], F32, tag="work", name="node_bank")
+                bias_bank = work.tile([P, TD], F32, tag="work", name="bias_bank")
+                for c, pick in ((0, pick_i[:, rt, :]), (HD, pick_j[:])):
+                    cols = slice(c, c + HD)
+                    nc.tensor.matmul(out=node_bank[:, cols], lhsT=pick, rhs=node_rows[:], start=True, stop=True)
+                    nc.tensor.matmul(
+                        out=bias_bank[:, cols], lhsT=ones[:], rhs=vec_rows[:, cols], start=True, stop=False
+                    )
+                    nc.tensor.matmul(out=bias_bank[:, cols], lhsT=pick, rhs=node_rows[:], start=False, stop=True)
+                nc.scalar.copy(out=z_in[:, rt, 0:TD], in_=node_bank[:])
+                nc.scalar.copy(out=bias_z[:, rt, 0:TD], in_=bias_bank[:])
 
         def multiply(b, halves):
             for gl in range(BATCH):
@@ -198,6 +220,7 @@ def tile_edgeupdaterwrapper_v01_pb_k_kernel(
         quantise(0)
         sort_words(2)
         quantise(1)
+        make_picks()
         for b in range(BATCHES):
             if b + HID_LEAD < BATCHES:
                 load_hid(b + HID_LEAD)
@@ -223,38 +246,39 @@ def tile_edgeupdaterwrapper_v01_pb_k_kernel(
         for b in late:
             load_words(b, range(1, HALVES))
 
-        bias_z = keep.tile([P, ROW_TILES, N1], F32)
         shift = keep.tile([P, ROW_TILES, N2], F32)
         for rt in range(ROW_TILES):
-            nc.vector.tensor_tensor(
-                out=bias_z[:, rt, :], in0=spread[:, VEC_B2 : VEC_B2 + N1], in1=z_in[:, rt, :], op=ALU.add
-            )
-            nc.vector.tensor_tensor(
-                out=shift[:, rt, :], in0=spread[:, VEC_B : VEC_B + N2], in1=z_in[:, rt, 2 * HD : N1], op=ALU.add
-            )
+            for out_tile, vec in ((bias_z[:, rt, TD:N1], VEC_B2 + TD), (shift[:, rt, :], VEC_B)):
+                nc.vector.tensor_tensor(
+                    out=out_tile, in0=spread[:, vec - TD : vec - TD + N2], in1=z_in[:, rt, TD:N1], op=ALU.add
+                )
 
         s_sorted = keep.tile([P, ROW_TILES, HALVES, PACK, P], BF16)
         s_grouped = keep.tile([P, HALVES, ROW_TILES, P * PACK], BF16, align_bytes=64)
         s_codes = keep.tile([P, HALVES, ROWS], U32, align_bytes=64)
         s_scales = keep.tile([P, HALVES, ROWS], U8, align_bytes=64)
 
-        def finish_s(h, rt):
+        def finish_s(h):
             cols = slice(h * BANK, (h + 1) * BANK)
-            summed = stage.tile([P, BANK], F32, name="summed")
-            nc.vector.tensor_tensor(out=summed[:], in0=acc[rt, h][:], in1=bias_z[:, rt, cols], op=ALU.add)
-            nc.vector.tensor_tensor(
-                out=s_sorted[:, rt, h, :, :].rearrange("p t q -> p q t"),
-                in0=summed[:].rearrange("p (q t) -> p q t", t=PACK),
-                in1=z_in[:, rt, cols].rearrange("p (q t) -> p q t", t=PACK),
-                op=ALU.max,
-            )
-            s_flipped = work.tile([P, PACK, P], BF16, tag="work", name="s_flipped")
-            for t in range(PACK):
-                nc.tensor.transpose(s_flipped[:, t, :], s_sorted[:, rt, h, t, :], ident_bf16[:])
-            nc.scalar.copy(
-                out=s_grouped[:, h, rt, :].rearrange("p (r t) -> p r t", t=PACK),
-                in_=s_flipped[:].rearrange("p t r -> p r t"),
-            )
+            sums = {}
+            for rt in range(ROW_TILES):
+                summed = stage.tile([P, BANK], F32, name="summed")
+                nc.vector.tensor_tensor(out=summed[:], in0=acc[rt, h][:], in1=bias_z[:, rt, cols], op=ALU.add)
+                sums[rt] = summed
+            for rt in range(ROW_TILES):
+                nc.vector.tensor_tensor(
+                    out=s_sorted[:, rt, h, :, :].rearrange("p t q -> p q t"),
+                    in0=sums[rt][:].rearrange("p (q t) -> p q t", t=PACK),
+                    in1=z_in[:, rt, cols].rearrange("p (q t) -> p q t", t=PACK),
+                    op=ALU.max,
+                )
+                s_flipped = work.tile([P, PACK, P], BF16, tag="work", name="s_flipped")
+                for t in range(PACK):
+                    nc.tensor.transpose(s_flipped[:, t, :], s_sorted[:, rt, h, t, :], ident_bf16[:])
+                nc.scalar.copy(
+                    out=s_grouped[:, h, rt, :].rearrange("p (r t) -> p r t", t=PACK),
+                    in_=s_flipped[:].rearrange("p t r -> p r t"),
+                )
 
         def quantise_s(h, rt):
             rows = slice(rt * P, (rt + 1) * P)
@@ -281,8 +305,7 @@ def tile_edgeupdaterwrapper_v01_pb_k_kernel(
 
         multiply(late[0], range(1, HALVES))
         for h in range(HALVES):
-            for rt in range(ROW_TILES):
-                finish_s(h, rt)
+            finish_s(h)
             for rt in range(ROW_TILES):
                 quantise_s(h, rt)
             if h == 0:
@@ -290,46 +313,55 @@ def tile_edgeupdaterwrapper_v01_pb_k_kernel(
                     multiply(b, range(1, HALVES))
             second_product(h)
 
-        z_tiles = {}
-        stats = {}
-        for rt in range(ROW_TILES):
-            z = keep.tile([P, N2], F32, name="z%d" % rt)
-            z_sum = keep.tile([P, 1], F32, name="z_sum%d" % rt)
-            neg_mean = keep.tile([P, 1], F32, name="neg_mean%d" % rt)
-            result = keep.tile([P, N2], F32, name="result%d" % rt)
-            square_sum = keep.tile([P, 1], F32, name="square_sum%d" % rt)
-            std = keep.tile([P, 1], F32, name="std%d" % rt)
-            nc.vector.scalar_tensor_tensor(
-                out=z[:],
-                in0=z_acc[rt][:],
-                scalar=1.0,
-                in1=spread[:, VEC_BO : VEC_BO + N2],
-                op0=ALU.mult,
-                op1=ALU.add,
-                accum_out=z_sum[:],
-            )
-            nc.vector.tensor_scalar_mul(out=neg_mean[:], in0=z_sum[:], scalar1=-1.0 / N2)
+        def column(name):
+            return [keep.tile([P, 1], F32, name="%s%d" % (name, rt)) for rt in range(ROW_TILES)]
+
+        def row(name):
+            return [keep.tile([P, N2], F32, name="%s%d" % (name, rt)) for rt in range(ROW_TILES)]
+
+        z_sum, neg_mean, square_sum, rstd = column("z_sum"), column("neg_mean"), column("square_sum"), column("rstd")
+        z, centred, result = row("z"), row("centred"), row("result")
+
+        def negate_mean(rt):
+            nc.scalar.mul(out=neg_mean[rt][:], in_=z_sum[rt][:], mul=-1.0 / N2)
+
+        def sum_squares(rt):
             nc.scalar.activation(
-                out=result[:], in_=z[:], func=ACT.Square, bias=neg_mean[:], scale=1.0, accum_out=square_sum[:]
+                out=result[rt][:], in_=z[rt][:], func=ACT.Square, bias=neg_mean[rt][:], accum_out=square_sum[rt][:]
             )
-            nc.scalar.activation(out=std[:], in_=square_sum[:], func=ACT.Sqrt, bias=eps[:], scale=1.0 / N2)
-            z_tiles[rt] = z
-            stats[rt] = (neg_mean, std, result)
+
+        def invert_std(rt):
+            nc.scalar.activation(
+                out=rstd[rt][:], in_=square_sum[rt][:], func=ACT.Abs_reciprocal_sqrt, bias=eps[:], scale=1.0 / N2
+            )
 
         for rt in range(ROW_TILES):
-            neg_mean, std, result = stats[rt]
-            centred = keep.tile([P, N2], F32, name="centred%d" % rt)
-            rstd = keep.tile([P, 1], F32, name="rstd%d" % rt)
             nc.vector.scalar_tensor_tensor(
-                out=centred[:],
-                in0=z_tiles[rt][:],
-                scalar=neg_mean[:],
-                in1=spread[:, VEC_G : VEC_G + N2],
+                out=z[rt][:],
+                in0=z_acc[rt][:],
+                scalar=1.0,
+                in1=spread[:, VEC_BO - TD : VEC_BO - TD + N2],
+                op0=ALU.mult,
+                op1=ALU.add,
+                accum_out=z_sum[rt][:],
+            )
+        negate_mean(0)
+        sum_squares(0)
+        negate_mean(1)
+        invert_std(0)
+        sum_squares(1)
+        invert_std(1)
+        for rt in range(ROW_TILES):
+            nc.vector.scalar_tensor_tensor(
+                out=centred[rt][:],
+                in0=z[rt][:],
+                scalar=neg_mean[rt][:],
+                in1=spread[:, VEC_G - TD : VEC_G - TD + N2],
                 op0=ALU.add,
                 op1=ALU.mult,
             )
-            nc.vector.reciprocal(out=rstd[:], in_=std[:])
+        for rt in range(ROW_TILES):
             nc.vector.scalar_tensor_tensor(
-                out=result[:], in0=centred[:], scalar=rstd[:], in1=shift[:, rt, :], op0=ALU.mult, op1=ALU.add
+                out=result[rt][:], in0=centred[rt][:], scalar=rstd[rt][:], in1=shift[:, rt, :], op0=ALU.mult, op1=ALU.add
             )
-            nc.sync.dma_start(out=out_rows[rt * P : (rt + 1) * P, :], in_=result[:])
+            nc.sync.dma_start(out=out_rows[rt * P : (rt + 1) * P, :], in_=result[rt][:])

@@ -38,6 +38,7 @@ LATE_BATCHES = 2
 MAIN_BATCHES = BATCHES - LATE_BATCHES
 HID_LEAD = 3
 
+SYNC_SCALES = 2
 SPREAD_AFTER = 2
 
 FLOPS = 2 * ROWS * K1 * N1 + 2 * ROWS * N1 * N2
@@ -88,12 +89,15 @@ def tile_edgeupdaterwrapper_v01_pb_k_kernel(
         make_identity(nc, ident_f32[:])
         make_identity(nc, ident_bf16[:])
 
-        for b in range(BATCHES):
+        def load_scales(queue, b, view):
             for quad in range(4):
-                nc.gpsimd.dma_start(
-                    out=w2_planes[32 * quad : 32 * quad + PACK * PLANES, b, :].bitcast(F32),
-                    in_=W2_scales[b * BATCH : (b + 1) * BATCH, 4 * quad : 4 * quad + 4, :].bitcast(F32),
+                queue.dma_start(
+                    out=w2_planes[32 * quad : 32 * quad + PACK * PLANES, b, :].bitcast(view),
+                    in_=W2_scales[b * BATCH : (b + 1) * BATCH, 4 * quad : 4 * quad + 4, :].bitcast(view),
                 )
+
+        for b in range(SYNC_SCALES, BATCHES):
+            load_scales(nc.gpsimd, b, F32)
 
         z_in = keep.tile([P, ROW_TILES, N1], BF16)
         nc.gpsimd.dma_start(out=z_in[:, :, TD:N1], in_=p_ln_rows)
@@ -211,6 +215,8 @@ def tile_edgeupdaterwrapper_v01_pb_k_kernel(
 
         for b in range(HID_LEAD):
             load_hid(b)
+            if b == 0:
+                load_scales(nc.sync, 0, I32)
         load_words(0, own_halves(0))
 
         sort_words(0)
@@ -225,6 +231,8 @@ def tile_edgeupdaterwrapper_v01_pb_k_kernel(
             if b + HID_LEAD < BATCHES:
                 load_hid(b + HID_LEAD)
             if b + 1 < BATCHES:
+                if b + 1 < SYNC_SCALES:
+                    load_scales(nc.sync, b + 1, I32)
                 load_words(b + 1, own_halves(b + 1))
             if b + 2 < BATCHES:
                 flip(b + 2)

@@ -36,8 +36,11 @@ PLANES = 4
 W2_BUFS = 3 * BATCH
 LATE_BATCHES = 2
 MAIN_BATCHES = BATCHES - LATE_BATCHES
-HID_LEAD = 3
-
+LAST = BATCHES - 1
+CHUNKS = 2
+CHUNK = BANK // CHUNKS
+HID_LEAD = 4
+FLIP_LEAD = 2
 SYNC_SCALES = 2
 SPREAD_AFTER = 2
 
@@ -100,8 +103,6 @@ def tile_edgeupdaterwrapper_v01_pb_k_kernel(
             load_scales(nc.gpsimd, b, F32)
 
         z_in = keep.tile([P, ROW_TILES, N1], BF16)
-        nc.gpsimd.dma_start(out=z_in[:, :, TD:N1], in_=p_ln_rows)
-
         hid_codes = keep.tile([P, PASSES1 * ROWS], U32, align_bytes=64)
         hid_scales = keep.tile([P, PASSES1 * ROWS], U8, align_bytes=64)
         wo_words = keep.tile([P, PASSES2, N2], I32, align_bytes=64)
@@ -210,8 +211,17 @@ def tile_edgeupdaterwrapper_v01_pb_k_kernel(
                             rhs=w2_tiles[g][:, cols].bitcast(FP8X4),
                             rhs_scale=w2_planes[PACK * gl : P, b, cols],
                             start=(g == 0),
-                            stop=(g == PASSES1 - 1),
+                            stop=(g == (PASSES1 if h == 0 else LAST * BATCH) - 1),
                         )
+
+        def load_last_operands():
+            nc.sync.dma_start(out=wo_words[:], in_=Wo_words.rearrange("g p n t -> p g (n t)").bitcast(I32))
+            for quad in range(4):
+                nc.sync.dma_start(
+                    out=wo_planes[32 * quad : 32 * quad + PACK * PASSES2, :].bitcast(I32),
+                    in_=Wo_scales[:, 4 * quad : 4 * quad + 4, :].bitcast(I32),
+                )
+            nc.sync.dma_start(out=z_in[:, :, TD:N1], in_=p_ln_rows)
 
         for b in range(HID_LEAD):
             load_hid(b)
@@ -220,39 +230,63 @@ def tile_edgeupdaterwrapper_v01_pb_k_kernel(
         load_words(0, own_halves(0))
 
         sort_words(0)
-        flip(0)
-        sort_words(1)
-        flip(1)
-        quantise(0)
-        sort_words(2)
-        quantise(1)
+        for b in range(FLIP_LEAD):
+            flip(b)
+            sort_words(b + 1)
+            quantise(b)
         make_picks()
         for b in range(BATCHES):
             if b + HID_LEAD < BATCHES:
                 load_hid(b + HID_LEAD)
+            elif b + HID_LEAD == BATCHES:
+                load_last_operands()
             if b + 1 < BATCHES:
                 if b + 1 < SYNC_SCALES:
                     load_scales(nc.sync, b + 1, I32)
                 load_words(b + 1, own_halves(b + 1))
-            if b + 2 < BATCHES:
-                flip(b + 2)
+            if b + FLIP_LEAD < BATCHES:
+                flip(b + FLIP_LEAD)
             multiply(b, own_halves(b))
             if b == SPREAD_AFTER:
                 spread_vectors()
-            if b + 3 < BATCHES:
-                sort_words(b + 3)
-            if b + 2 < BATCHES:
-                quantise(b + 2)
+            if b + FLIP_LEAD < BATCHES:
+                quantise(b + FLIP_LEAD)
+            if b + FLIP_LEAD + 1 < BATCHES:
+                sort_words(b + FLIP_LEAD + 1)
 
-        nc.sync.dma_start(out=wo_words[:], in_=Wo_words.rearrange("g p n t -> p g (n t)").bitcast(I32))
-        for quad in range(4):
-            nc.sync.dma_start(
-                out=wo_planes[32 * quad : 32 * quad + PACK * PASSES2, :].bitcast(I32),
-                in_=Wo_scales[:, 4 * quad : 4 * quad + 4, :].bitcast(I32),
-            )
-        late = range(MAIN_BATCHES, BATCHES)
+        late = range(MAIN_BATCHES, LAST)
         for b in late:
             load_words(b, range(1, HALVES))
+        last_words = keep.tile([P, BATCH, BANK], I32, align_bytes=64)
+        for c in range(CHUNKS):
+            for gl in range(0, BATCH, 2):
+                g = LAST * BATCH + gl
+                nc.sync.dma_start(
+                    out=last_words[:, gl : gl + 2, c * CHUNK : (c + 1) * CHUNK],
+                    in_=W2_words[g : g + 2, :, BANK + c * CHUNK : BANK + (c + 1) * CHUNK, :]
+                    .rearrange("g p n t -> p g (n t)")
+                    .bitcast(I32),
+                )
+
+        last_acc = {}
+
+        def multiply_last(c):
+            cols = slice(c * CHUNK, (c + 1) * CHUNK)
+            for rt in range(ROW_TILES):
+                last_acc[c, rt] = work.tile([P, CHUNK], F32, tag="work", name="last_acc")
+            for gl in range(BATCH):
+                g = LAST * BATCH + gl
+                for rt in range(ROW_TILES):
+                    rows = slice(g * ROWS + rt * P, g * ROWS + (rt + 1) * P)
+                    nc.tensor.matmul_mx(
+                        out=last_acc[c, rt][:],
+                        lhsT=hid_codes[:, rows].bitcast(FP8X4),
+                        lhsT_scale=hid_scales[:, rows],
+                        rhs=last_words[:, gl, cols].bitcast(FP8X4),
+                        rhs_scale=w2_planes[PACK * gl : P, LAST, BANK + c * CHUNK : BANK + (c + 1) * CHUNK],
+                        start=(gl == 0),
+                        stop=(gl == BATCH - 1),
+                    )
 
         shift = keep.tile([P, ROW_TILES, N2], F32)
         for rt in range(ROW_TILES):
@@ -266,21 +300,25 @@ def tile_edgeupdaterwrapper_v01_pb_k_kernel(
         s_codes = keep.tile([P, HALVES, ROWS], U32, align_bytes=64)
         s_scales = keep.tile([P, HALVES, ROWS], U8, align_bytes=64)
 
-        def finish_s(h):
-            cols = slice(h * BANK, (h + 1) * BANK)
+        def add_up(parts, h, first, width):
+            cols = slice(h * BANK + first, h * BANK + first + width)
+            places = slice(first // PACK, (first + width) // PACK)
             sums = {}
             for rt in range(ROW_TILES):
                 summed = stage.tile([P, BANK], F32, name="summed")
-                nc.vector.tensor_tensor(out=summed[:], in0=acc[rt, h][:], in1=bias_z[:, rt, cols], op=ALU.add)
+                nc.vector.tensor_tensor(out=summed[:, 0:width], in0=parts[rt][:], in1=bias_z[:, rt, cols], op=ALU.add)
                 sums[rt] = summed
             for rt in range(ROW_TILES):
                 nc.vector.tensor_tensor(
-                    out=s_sorted[:, rt, h, :, :].rearrange("p t q -> p q t"),
-                    in0=sums[rt][:].rearrange("p (q t) -> p q t", t=PACK),
+                    out=s_sorted[:, rt, h, :, places].rearrange("p t q -> p q t"),
+                    in0=sums[rt][:, 0:width].rearrange("p (q t) -> p q t", t=PACK),
                     in1=z_in[:, rt, cols].rearrange("p (q t) -> p q t", t=PACK),
                     op=ALU.max,
                 )
-                s_flipped = work.tile([P, PACK, P], BF16, tag="work", name="s_flipped")
+
+        def flip_s(h):
+            for rt in range(ROW_TILES):
+                s_flipped = acc_pool.tile([P, PACK, P], BF16, name="acc%d%d" % (rt, h))
                 for t in range(PACK):
                     nc.tensor.transpose(s_flipped[:, t, :], s_sorted[:, rt, h, t, :], ident_bf16[:])
                 nc.scalar.copy(
@@ -300,7 +338,7 @@ def tile_edgeupdaterwrapper_v01_pb_k_kernel(
             for rt in range(ROW_TILES):
                 rows = slice(rt * P, (rt + 1) * P)
                 if h == 0:
-                    z_acc[rt] = work.tile([P, N2], F32, tag="work", name="z_acc")
+                    z_acc[rt] = acc_pool.tile([P, N2], F32, name="acc%d0" % rt)
                 nc.tensor.matmul_mx(
                     out=z_acc[rt][:],
                     lhsT=s_codes[:, h, rows].bitcast(FP8X4),
@@ -311,15 +349,23 @@ def tile_edgeupdaterwrapper_v01_pb_k_kernel(
                     stop=(h == PASSES2 - 1),
                 )
 
-        multiply(late[0], range(1, HALVES))
-        for h in range(HALVES):
-            finish_s(h)
-            for rt in range(ROW_TILES):
-                quantise_s(h, rt)
-            if h == 0:
-                for b in late[1:]:
-                    multiply(b, range(1, HALVES))
-            second_product(h)
+        for b in late:
+            multiply(b, range(1, HALVES))
+        add_up([acc[rt, 0] for rt in range(ROW_TILES)], 0, 0, BANK)
+        flip_s(0)
+        for rt in range(ROW_TILES):
+            cols = slice(BANK, N1)
+            nc.vector.tensor_tensor(out=bias_z[:, rt, cols], in0=acc[rt, 1][:], in1=bias_z[:, rt, cols], op=ALU.add)
+        for rt in range(ROW_TILES):
+            quantise_s(0, rt)
+        for c in range(CHUNKS):
+            multiply_last(c)
+            add_up([last_acc[c, rt] for rt in range(ROW_TILES)], 1, c * CHUNK, CHUNK)
+        second_product(0)
+        flip_s(1)
+        for rt in range(ROW_TILES):
+            quantise_s(1, rt)
+        second_product(1)
 
         def column(name):
             return [keep.tile([P, 1], F32, name="%s%d" % (name, rt)) for rt in range(ROW_TILES)]

@@ -39,7 +39,7 @@ MAIN_BATCHES = BATCHES - LATE_BATCHES
 LAST = BATCHES - 1
 CHUNKS = 2
 CHUNK = BANK // CHUNKS
-HID_LEAD = 4
+HID_LEAD = 3
 FLIP_LEAD = 2
 SYNC_SCALES = 2
 SPREAD_AFTER = 2
@@ -197,8 +197,8 @@ def tile_edgeupdaterwrapper_v01_pb_k_kernel(
                 nc.scalar.copy(out=z_in[:, rt, 0:TD], in_=node_bank[:])
                 nc.scalar.copy(out=bias_z[:, rt, 0:TD], in_=bias_bank[:])
 
-        def multiply(b, halves):
-            for gl in range(BATCH):
+        def multiply(b, halves, passes=range(BATCH)):
+            for gl in passes:
                 g = b * BATCH + gl
                 for rt in range(ROW_TILES):
                     rows = slice(g * ROWS + rt * P, g * ROWS + (rt + 1) * P)
@@ -244,9 +244,10 @@ def tile_edgeupdaterwrapper_v01_pb_k_kernel(
                 if b + 1 < SYNC_SCALES:
                     load_scales(nc.sync, b + 1, I32)
                 load_words(b + 1, own_halves(b + 1))
+            multiply(b, own_halves(b), range(BATCH // 2))
             if b + FLIP_LEAD < BATCHES:
                 flip(b + FLIP_LEAD)
-            multiply(b, own_halves(b))
+            multiply(b, own_halves(b), range(BATCH // 2, BATCH))
             if b == SPREAD_AFTER:
                 spread_vectors()
             if b + FLIP_LEAD < BATCHES:

from contextlib import ExitStack

import concourse.mybir as mybir
from concourse.masks import make_identity

F32 = mybir.dt.float32
BF16 = mybir.dt.bfloat16
I32 = mybir.dt.int32
U32 = mybir.dt.uint32
U8 = mybir.dt.uint8
FP8X4 = mybir.dt.float8_e4m3fn_x4
ALU = mybir.AluOpType
ACT = mybir.ActivationFunctionType

P = 128
PACK = 4
K_PASS = P * PACK
BANK = 512

ROWS = 256
ROW_TILES = ROWS // P
NODES = 16
HD = 256
TD = 2 * HD
K1 = 16384
N1 = 1024
N2 = 512
PASSES1 = K1 // K_PASS
PASSES2 = N1 // K_PASS
HALVES = N1 // BANK
EPS = 1e-5

BATCH = 4
BATCHES = PASSES1 // BATCH
PLANES = 4
W2_BUFS = 3 * BATCH
LATE_BATCHES = 2
MAIN_BATCHES = BATCHES - LATE_BATCHES
LAST = BATCHES - 1
CHUNKS = 2
CHUNK = BANK // CHUNKS
HID_LEAD = 3
FLIP_LEAD = 2
SYNC_SCALES = 2
SPREAD_AFTER = 2

FLOPS = 2 * ROWS * K1 * N1 + 2 * ROWS * N1 * N2


def tile_edgeupdaterwrapper_v01_pb_k_kernel(
    tc, hid, x_down, p_ln, W2_words, W2_scales, b2, Wo_words, Wo_scales, bo, ln_out_g, ln_out_b, out
):
    nc = tc.nc
    hid_rows = hid.rearrange("b i j k -> (b i j) k").rearrange("(t p) k -> p t k", p=P)
    p_ln_rows = p_ln.rearrange("b i j f -> (b i j) f").rearrange("(t p) f -> p t f", p=P)
    out_rows = out.rearrange("b i j f -> (b i j) f")

    with ExitStack() as ctx:
        ctx.enter_context(tc.manual_schedule())
        keep = ctx.enter_context(tc.tile_pool(name="keep", bufs=1))
        raw_pool = ctx.enter_context(tc.tile_pool(name="raw", bufs=HID_LEAD + 1))
        stage = ctx.enter_context(tc.tile_pool(name="stage", bufs=2))
        w2_pool = ctx.enter_context(tc.tile_pool(name="w2", bufs=W2_BUFS))
        acc_pool = ctx.enter_context(tc.psum_pool(name="acc", bufs=1))
        work = ctx.enter_context(tc.psum_pool(name="work", bufs=4))

        w2_planes = keep.tile([P, BATCHES, N1], U8, align_bytes=64)
        wo_planes = keep.tile([P, N2], U8, align_bytes=64)
        eps = keep.tile([P, 1], F32)
        nc.vector.memset(eps[:], EPS)
        table_warm = keep.tile([P, 1], F32)
        nc.scalar.activation(out=table_warm[:], in_=eps[:], func=ACT.Abs_reciprocal_sqrt)
        nc.vector.memset(w2_planes[:].bitcast(I32), 0)
        nc.vector.memset(wo_planes[:].bitcast(I32), 0)

        VEC_B2, VEC_BO, VEC_G, VEC_B = 0, N1, N1 + N2, N1 + 2 * N2
        VEC_COLS = N1 + 3 * N2
        vec_rows = keep.tile([P, VEC_COLS], BF16)
        ones = keep.tile([P, P], BF16)
        node_rows = keep.tile([P, HD], BF16)
        nc.vector.memset(node_rows[:], 0.0)
        nc.vector.memset(vec_rows[:], 0.0)
        nc.vector.memset(ones[:], 1.0)
        nc.scalar.dma_start(out=vec_rows[0:1, VEC_B2 : VEC_B2 + N1], in_=b2.unsqueeze(0))
        nc.scalar.dma_start(out=vec_rows[0:1, VEC_BO : VEC_BO + N2], in_=bo.unsqueeze(0))
        nc.scalar.dma_start(out=vec_rows[0:1, VEC_G : VEC_G + N2], in_=ln_out_g.unsqueeze(0))
        nc.scalar.dma_start(out=vec_rows[0:1, VEC_B : VEC_B + N2], in_=ln_out_b.unsqueeze(0))
        nc.scalar.dma_start(out=node_rows[0:NODES, :], in_=x_down[0, :, :])

        ident_f32 = keep.tile([P, P], F32)
        ident_bf16 = keep.tile([P, P], BF16)
        make_identity(nc, ident_f32[:])
        make_identity(nc, ident_bf16[:])

        def load_scales(queue, b, view):
            for quad in range(4):
                queue.dma_start(
                    out=w2_planes[32 * quad : 32 * quad + PACK * PLANES, b, :].bitcast(view),
                    in_=W2_scales[b * BATCH : (b + 1) * BATCH, 4 * quad : 4 * quad + 4, :].bitcast(view),
                )

        for b in range(SYNC_SCALES, BATCHES):
            load_scales(nc.gpsimd, b, F32)

        z_in = keep.tile([P, ROW_TILES, N1], BF16)
        hid_codes = keep.tile([P, PASSES1 * ROWS], U32, align_bytes=64)
        hid_scales = keep.tile([P, PASSES1 * ROWS], U8, align_bytes=64)
        wo_words = keep.tile([P, PASSES2, N2], I32, align_bytes=64)
        raw_tiles = {}
        sorted_tiles = {}
        grouped_tiles = {}
        w2_tiles = {}
        acc = {}
        for rt in range(ROW_TILES):
            for h in range(HALVES):
                acc[rt, h] = acc_pool.tile([P, BANK], F32, name="acc%d%d" % (rt, h))

        def load_hid(b):
            raw = raw_pool.tile([P, ROW_TILES, BATCH * K_PASS], BF16)
            nc.sync.dma_start(out=raw[:], in_=hid_rows[:, :, b * BATCH * K_PASS : (b + 1) * BATCH * K_PASS])
            raw_tiles[b] = raw

        def own_halves(b):
            return range(HALVES) if b < MAIN_BATCHES else range(1)

        def load_words(b, halves):
            cols = slice(halves[0] * BANK, (halves[-1] + 1) * BANK)
            for g in range(b * BATCH, (b + 1) * BATCH):
                if g not in w2_tiles:
                    w2_words = w2_pool.tile([P, N1], I32, align_bytes=64)
                    w2_tiles[g] = w2_words
                nc.sync.dma_start(
                    out=w2_tiles[g][:, cols],
                    in_=W2_words[g, :, cols, :].rearrange("p n t -> p (n t)").bitcast(I32),
                )

        def sort_words(b):
            words = stage.tile([P, ROW_TILES, BATCH, 2, P], F32, name="sorted_words")
            nc.vector.tensor_copy(
                out=words[:].rearrange("p t g u q -> p t g q u"),
                in_=raw_tiles[b][:].bitcast(F32).rearrange("p t (g q u) -> p t g q u", q=P, u=2),
            )
            sorted_tiles[b] = words

        def flip(b):
            grouped = stage.tile([P, BATCH * ROWS * PACK], BF16, align_bytes=64, name="grouped")
            pairs = grouped[:].bitcast(F32).rearrange("p (g r u) -> p g r u", r=ROWS, u=2)
            for gl in range(BATCH):
                flipped = work.tile([P, 2, ROWS], F32, tag="work", name="flipped")
                for u in range(2):
                    for rt in range(ROW_TILES):
                        nc.tensor.transpose(
                            flipped[:, u, rt * P : (rt + 1) * P], sorted_tiles[b][:, rt, gl, u, :], ident_f32[:]
                        )
                nc.scalar.copy(out=pairs[:, gl, :, :], in_=flipped[:].rearrange("p u r -> p r u"))
            grouped_tiles[b] = grouped

        def quantise(b):
            cols = slice(b * BATCH * ROWS, (b + 1) * BATCH * ROWS)
            nc.vector.quantize_mx(
                out=hid_codes[:, cols].bitcast(FP8X4), scales=hid_scales[:, cols], in_=grouped_tiles[b][:]
            )

        bias_z = keep.tile([P, ROW_TILES, N1], F32)
        spread = keep.tile([P, VEC_COLS - TD], F32)
        pick_i = keep.tile([P, ROW_TILES, P], BF16)
        pick_j = keep.tile([P, P], BF16)
        nodes_per_tile = P // NODES

        def make_picks():
            nc.vector.tensor_copy(
                out=pick_j[:].rearrange("n (a c) -> n a c", c=NODES),
                in_=ident_bf16[:, 0:NODES].unsqueeze(1).to_broadcast([P, nodes_per_tile, NODES]),
            )
            for rt in range(ROW_TILES):
                own = ident_bf16[:, rt * nodes_per_tile : (rt + 1) * nodes_per_tile]
                nc.vector.tensor_copy(
                    out=pick_i[:, rt, :].rearrange("n (a c) -> n a c", c=NODES),
                    in_=own.unsqueeze(2).to_broadcast([P, nodes_per_tile, NODES]),
                )

        def spread_vectors():
            for c in range(TD, VEC_COLS, BANK):
                row_bank = work.tile([P, BANK], F32, tag="work", name="row_bank")
                nc.tensor.matmul(out=row_bank[:], lhsT=ones[:], rhs=vec_rows[:, c : c + BANK], start=True, stop=True)
                nc.scalar.copy(out=spread[:, c - TD : c - TD + BANK], in_=row_bank[:])
            for rt in range(ROW_TILES):
                node_bank = work.tile([P, TD], F32, tag="work", name="node_bank")
                bias_bank = work.tile([P, TD], F32, tag="work", name="bias_bank")
                for c, pick in ((0, pick_i[:, rt, :]), (HD, pick_j[:])):
                    cols = slice(c, c + HD)
                    nc.tensor.matmul(out=node_bank[:, cols], lhsT=pick, rhs=node_rows[:], start=True, stop=True)
                    nc.tensor.matmul(
                        out=bias_bank[:, cols], lhsT=ones[:], rhs=vec_rows[:, cols], start=True, stop=False
                    )
                    nc.tensor.matmul(out=bias_bank[:, cols], lhsT=pick, rhs=node_rows[:], start=False, stop=True)
                nc.scalar.copy(out=z_in[:, rt, 0:TD], in_=node_bank[:])
                nc.scalar.copy(out=bias_z[:, rt, 0:TD], in_=bias_bank[:])

        def multiply(b, halves, passes=range(BATCH)):
            for gl in passes:
                g = b * BATCH + gl
                for rt in range(ROW_TILES):
                    rows = slice(g * ROWS + rt * P, g * ROWS + (rt + 1) * P)
                    for h in halves:
                        cols = slice(h * BANK, (h + 1) * BANK)
                        nc.tensor.matmul_mx(
                            out=acc[rt, h][:],
                            lhsT=hid_codes[:, rows].bitcast(FP8X4),
                            lhsT_scale=hid_scales[:, rows],
                            rhs=w2_tiles[g][:, cols].bitcast(FP8X4),
                            rhs_scale=w2_planes[PACK * gl : P, b, cols],
                            start=(g == 0),
                            stop=(g == (PASSES1 if h == 0 else LAST * BATCH) - 1),
                        )

        def load_last_operands():
            nc.sync.dma_start(out=wo_words[:], in_=Wo_words.rearrange("g p n t -> p g (n t)").bitcast(I32))
            for quad in range(4):
                nc.sync.dma_start(
                    out=wo_planes[32 * quad : 32 * quad + PACK * PASSES2, :].bitcast(I32),
                    in_=Wo_scales[:, 4 * quad : 4 * quad + 4, :].bitcast(I32),
                )
            nc.sync.dma_start(out=z_in[:, :, TD:N1], in_=p_ln_rows)

        for b in range(HID_LEAD):
            load_hid(b)
            if b == 0:
                load_scales(nc.sync, 0, I32)
        load_words(0, own_halves(0))

        sort_words(0)
        for b in range(FLIP_LEAD):
            flip(b)
            sort_words(b + 1)
            quantise(b)
        make_picks()
        for b in range(BATCHES):
            if b + HID_LEAD < BATCHES:
                load_hid(b + HID_LEAD)
            elif b + HID_LEAD == BATCHES:
                load_last_operands()
            if b + 1 < BATCHES:
                if b + 1 < SYNC_SCALES:
                    load_scales(nc.sync, b + 1, I32)
                load_words(b + 1, own_halves(b + 1))
            multiply(b, own_halves(b), range(BATCH // 2))
            if b + FLIP_LEAD < BATCHES:
                flip(b + FLIP_LEAD)
            multiply(b, own_halves(b), range(BATCH // 2, BATCH))
            if b == SPREAD_AFTER:
                spread_vectors()
            if b + FLIP_LEAD < BATCHES:
                quantise(b + FLIP_LEAD)
            if b + FLIP_LEAD + 1 < BATCHES:
                sort_words(b + FLIP_LEAD + 1)

        late = range(MAIN_BATCHES, LAST)
        for b in late:
            load_words(b, range(1, HALVES))
        last_words = keep.tile([P, BATCH, BANK], I32, align_bytes=64)
        for c in range(CHUNKS):
            for gl in range(0, BATCH, 2):
                g = LAST * BATCH + gl
                nc.sync.dma_start(
                    out=last_words[:, gl : gl + 2, c * CHUNK : (c + 1) * CHUNK],
                    in_=W2_words[g : g + 2, :, BANK + c * CHUNK : BANK + (c + 1) * CHUNK, :]
                    .rearrange("g p n t -> p g (n t)")
                    .bitcast(I32),
                )

        last_acc = {}

        def multiply_last(c):
            cols = slice(c * CHUNK, (c + 1) * CHUNK)
            for rt in range(ROW_TILES):
                last_acc[c, rt] = work.tile([P, CHUNK], F32, tag="work", name="last_acc")
            for gl in range(BATCH):
                g = LAST * BATCH + gl
                for rt in range(ROW_TILES):
                    rows = slice(g * ROWS + rt * P, g * ROWS + (rt + 1) * P)
                    nc.tensor.matmul_mx(
                        out=last_acc[c, rt][:],
                        lhsT=hid_codes[:, rows].bitcast(FP8X4),
                        lhsT_scale=hid_scales[:, rows],
                        rhs=last_words[:, gl, cols].bitcast(FP8X4),
                        rhs_scale=w2_planes[PACK * gl : P, LAST, BANK + c * CHUNK : BANK + (c + 1) * CHUNK],
                        start=(gl == 0),
                        stop=(gl == BATCH - 1),
                    )

        shift = keep.tile([P, ROW_TILES, N2], F32)
        for rt in range(ROW_TILES):
            for out_tile, vec in ((bias_z[:, rt, TD:N1], VEC_B2 + TD), (shift[:, rt, :], VEC_B)):
                nc.vector.tensor_tensor(
                    out=out_tile, in0=spread[:, vec - TD : vec - TD + N2], in1=z_in[:, rt, TD:N1], op=ALU.add
                )

        s_sorted = keep.tile([P, ROW_TILES, HALVES, PACK, P], BF16)
        s_grouped = keep.tile([P, HALVES, ROW_TILES, P * PACK], BF16, align_bytes=64)
        s_codes = keep.tile([P, HALVES, ROWS], U32, align_bytes=64)
        s_scales = keep.tile([P, HALVES, ROWS], U8, align_bytes=64)

        def add_up(parts, h, first, width):
            cols = slice(h * BANK + first, h * BANK + first + width)
            places = slice(first // PACK, (first + width) // PACK)
            sums = {}
            for rt in range(ROW_TILES):
                summed = stage.tile([P, BANK], F32, name="summed")
                nc.vector.tensor_tensor(out=summed[:, 0:width], in0=parts[rt][:], in1=bias_z[:, rt, cols], op=ALU.add)
                sums[rt] = summed
            for rt in range(ROW_TILES):
                nc.vector.tensor_tensor(
                    out=s_sorted[:, rt, h, :, places].rearrange("p t q -> p q t"),
                    in0=sums[rt][:, 0:width].rearrange("p (q t) -> p q t", t=PACK),
                    in1=z_in[:, rt, cols].rearrange("p (q t) -> p q t", t=PACK),
                    op=ALU.max,
                )

        def flip_s(h):
            for rt in range(ROW_TILES):
                s_flipped = acc_pool.tile([P, PACK, P], BF16, name="acc%d%d" % (rt, h))
                for t in range(PACK):
                    nc.tensor.transpose(s_flipped[:, t, :], s_sorted[:, rt, h, t, :], ident_bf16[:])
                nc.scalar.copy(
                    out=s_grouped[:, h, rt, :].rearrange("p (r t) -> p r t", t=PACK),
                    in_=s_flipped[:].rearrange("p t r -> p r t"),
                )

        def quantise_s(h, rt):
            rows = slice(rt * P, (rt + 1) * P)
            nc.vector.quantize_mx(
                out=s_codes[:, h, rows].bitcast(FP8X4), scales=s_scales[:, h, rows], in_=s_grouped[:, h, rt, :]
            )

        z_acc = {}

        def second_product(h):
            for rt in range(ROW_TILES):
                rows = slice(rt * P, (rt + 1) * P)
                if h == 0:
                    z_acc[rt] = acc_pool.tile([P, N2], F32, name="acc%d0" % rt)
                nc.tensor.matmul_mx(
                    out=z_acc[rt][:],
                    lhsT=s_codes[:, h, rows].bitcast(FP8X4),
                    lhsT_scale=s_scales[:, h, rows],
                    rhs=wo_words[:, h, :].bitcast(FP8X4),
                    rhs_scale=wo_planes[PACK * h : P, :],
                    start=(h == 0),
                    stop=(h == PASSES2 - 1),
                )

        for b in late:
            multiply(b, range(1, HALVES))
        add_up([acc[rt, 0] for rt in range(ROW_TILES)], 0, 0, BANK)
        flip_s(0)
        for rt in range(ROW_TILES):
            cols = slice(BANK, N1)
            nc.vector.tensor_tensor(out=bias_z[:, rt, cols], in0=acc[rt, 1][:], in1=bias_z[:, rt, cols], op=ALU.add)
        for rt in range(ROW_TILES):
            quantise_s(0, rt)
        for c in range(CHUNKS):
            multiply_last(c)
            add_up([last_acc[c, rt] for rt in range(ROW_TILES)], 1, c * CHUNK, CHUNK)
        second_product(0)
        flip_s(1)
        for rt in range(ROW_TILES):
            quantise_s(1, rt)
        second_product(1)

        def column(name):
            return [keep.tile([P, 1], F32, name="%s%d" % (name, rt)) for rt in range(ROW_TILES)]

        def row(name):
            return [keep.tile([P, N2], F32, name="%s%d" % (name, rt)) for rt in range(ROW_TILES)]

        z_sum, neg_mean, square_sum, rstd = column("z_sum"), column("neg_mean"), column("square_sum"), column("rstd")
        z, centred, result = row("z"), row("centred"), row("result")

        def negate_mean(rt):
            nc.scalar.mul(out=neg_mean[rt][:], in_=z_sum[rt][:], mul=-1.0 / N2)

        def sum_squares(rt):
            nc.scalar.activation(
                out=result[rt][:], in_=z[rt][:], func=ACT.Square, bias=neg_mean[rt][:], accum_out=square_sum[rt][:]
            )

        def invert_std(rt):
            nc.scalar.activation(
                out=rstd[rt][:], in_=square_sum[rt][:], func=ACT.Abs_reciprocal_sqrt, bias=eps[:], scale=1.0 / N2
            )

        for rt in range(ROW_TILES):
            nc.vector.scalar_tensor_tensor(
                out=z[rt][:],
                in0=z_acc[rt][:],
                scalar=1.0,
                in1=spread[:, VEC_BO - TD : VEC_BO - TD + N2],
                op0=ALU.mult,
                op1=ALU.add,
                accum_out=z_sum[rt][:],
            )
        negate_mean(0)
        sum_squares(0)
        negate_mean(1)
        invert_std(0)
        sum_squares(1)
        invert_std(1)
        for rt in range(ROW_TILES):
            nc.vector.scalar_tensor_tensor(
                out=centred[rt][:],
                in0=z[rt][:],
                scalar=neg_mean[rt][:],
                in1=spread[:, VEC_G - TD : VEC_G - TD + N2],
                op0=ALU.add,
                op1=ALU.mult,
            )
        for rt in range(ROW_TILES):
            nc.vector.scalar_tensor_tensor(
                out=result[rt][:], in0=centred[rt][:], scalar=rstd[rt][:], in1=shift[:, rt, :], op0=ALU.mult, op1=ALU.add
            )
            nc.sync.dma_start(out=out_rows[rt * P : (rt + 1) * P, :], in_=result[rt][:])
